import numpy as np
import ml_dtypes


def mxq(x, axis, fmt="e4m3"):
    dtype, down = {"e4m3": (ml_dtypes.float8_e4m3fn, 7), "e5m2": (ml_dtypes.float8_e5m2, 14)}[fmt]
    v = np.moveaxis(np.asarray(x, np.float32).astype(ml_dtypes.bfloat16).astype(np.float64), axis, -1)
    blocks = v.reshape(v.shape[:-1] + (-1, 32))
    amax = np.abs(blocks).max(-1, keepdims=True)
    byte = np.maximum(np.where(amax > 0, np.frexp(amax)[1] - 1 + 127, 0) - down, 1)
    scale = np.exp2(byte - 127.0)
    codes = (blocks / scale).astype(np.float32).astype(dtype).astype(np.float64)
    return np.moveaxis((codes * scale).reshape(v.shape), -1, axis)


WIDE = False


def mx_kscale(k):
    if not WIDE:
        return np.ones(k)
    levels = np.array([10, -10, 5, -5, 0])
    if k % 512:
        return np.exp2(np.random.permutation(np.resize(levels, k // 32))).repeat(32)
    a = np.empty((k // 512, 16))
    for p in range(k // 512):
        a[p, :8] = np.random.permutation(np.resize(levels, 8))
        for g in range(8):
            far = levels[np.abs(levels - a[p, g]) >= 10]
            a[p, g + 8] = far[np.random.randint(len(far))]
    return np.exp2(a.ravel()).repeat(32)


BF16 = ml_dtypes.bfloat16


def bf(x):
    return np.asarray(x, np.float32).astype(BF16)


def f64(x):
    return np.asarray(x).astype(np.float64)


E2M1 = np.array([0.0, 0.5, 1.0, 1.5, 2.0, 3.0, 4.0, 6.0, -0.0, -0.5, -1.0, -1.5, -2.0, -3.0, -4.0, -6.0])


def pack_weight(w, fmt):
    k, n = w.shape
    w = f64(bf(w)).reshape(k // 32, 32, n)
    amax = np.abs(w).max(1)
    if fmt == "e4m3":
        byte = np.frexp(amax)[1] - 1 + 127 - 7
    else:
        mant, ex = np.frexp(amax / 6.0)
        byte = np.where(mant > 0.5, ex, ex - 1) + 127
    byte = np.clip(np.where(amax > 0, byte, 1), 1, 254)
    scaled = (w * np.exp2(127.0 - byte)[:, None, :]).reshape(k, n).astype(np.float32)
    by_word = np.ascontiguousarray(scaled.reshape(k // 512, 128, 4, n).transpose(0, 1, 3, 2))
    if fmt == "e4m3":
        words = by_word.astype(ml_dtypes.float8_e4m3fn).view(np.uint8)
    else:
        c = by_word.astype(ml_dtypes.float4_e2m1fn).view(np.uint8) & 0xF
        words = c[..., 0::2] | (c[..., 1::2] << 4)
    return np.ascontiguousarray(words), np.ascontiguousarray(byte.astype(np.uint8).reshape(k // 512, 16, n))


def unpack_weight(words, scales, fmt):
    g, p, n, _ = words.shape
    if fmt == "e4m3":
        vals = np.ascontiguousarray(words).view(ml_dtypes.float8_e4m3fn).astype(np.float64)
    else:
        nib = np.empty((g, p, n, 4), np.uint8)
        nib[..., 0::2] = words & 0xF
        nib[..., 1::2] = words >> 4
        vals = E2M1[nib]
    vals = vals * np.repeat(np.exp2(scales.astype(np.float64) - 127.0), 8, axis=1)[..., None]
    return vals.transpose(0, 1, 3, 2).reshape(g * 512, n)


B, T, S, Dt, Df = 8, 1024, 256, 512, 512
EPS = 1e-6


def rmsnorm(x, w):
    return x * (1.0 / np.sqrt(np.mean(x * x, axis=-1, keepdims=True) + EPS)) * w


def draw0():
    s = mx_kscale(Dt)
    t = mx_kscale(Df)
    text = bf(np.random.standard_normal((B, T, Dt)) * s)
    words, scales = pack_weight((np.random.standard_normal((Df, Dt)) / np.sqrt(Dt) / s[None, :]).T, "e4m3")
    return {"text": text,
            "Wq_w_words": words,
            "Wq_w_scales": scales,
            "Wq_b": bf(np.random.standard_normal(Df) * 0.3),
            "qn_w": bf((1.0 + 0.1 * np.random.standard_normal(Df)) * t),
            "k_norm": bf(np.random.standard_normal((B, S, Df)) / t)}


def core(text, Wq_w_words, Wq_w_scales, Wq_b, qn_w, k_norm):
    q = (mxq(f64(text), 2, "e4m3") @ unpack_weight(Wq_w_words, Wq_w_scales, "e4m3")) + f64(Wq_b)
    q = rmsnorm(q, f64(qn_w))
    scale = 1.0 / np.sqrt(Df)
    return (mxq(q, 2, "e4m3") @ mxq(f64(k_norm), 2, "e4m3").transpose(0, 2, 1)) * scale


def e4m3fn_bytes(y):
    return np.clip(np.asarray(y, np.float64), -448.0, 448.0).astype(np.float32).astype(ml_dtypes.float8_e4m3fn).view(np.uint8)


def e4m3fn_values(b):
    return np.asarray(b, np.uint8).view(ml_dtypes.float8_e4m3fn).astype(np.float64)


def setup_inputs():
    d = draw0()
    x0 = np.asarray(d['text']).astype(np.float64)
    s = (np.max(np.abs(x0), axis=(0, 1), keepdims=True) / 448.0).astype(np.float32)
    out = {}
    for k, v in d.items():
        if k == 'text':
            out['text_bytes'] = e4m3fn_bytes(x0 / s.astype(np.float64))
            out['text_scale'] = s
        else:
            out[k] = v
    return out


def reference(text_bytes, text_scale, Wq_w_words, Wq_w_scales, Wq_b, qn_w, k_norm):
    return core(e4m3fn_values(text_bytes) * text_scale.astype(np.float64), Wq_w_words, Wq_w_scales, Wq_b, qn_w, k_norm)

@@ -1,0 +1,320 @@
+from contextlib import ExitStack
+
+import concourse.mybir as mybir
+from concourse.masks import make_identity
+
+B, T, S, K, F = 8, 1024, 256, 512, 512
+EPS = 1e-6
+FLOPS = 2 * B * T * K * F + 2 * B * T * F * S
+
+F32 = mybir.dt.float32
+BF16 = mybir.dt.bfloat16
+I32 = mybir.dt.int32
+U32 = mybir.dt.uint32
+U8 = mybir.dt.uint8
+F8 = mybir.dt.float8_e4m3fn
+FP8X4 = mybir.dt.float8_e4m3fn_x4
+ALU = mybir.AluOpType
+ACT = mybir.ActivationFunctionType
+AXIS = mybir.AxisListType
+
+P = 128
+GT = 512
+NG = B * T // GT
+TILES = GT // P
+
+
+def tile_crossattention_pb_t_w8_kernel(
+    tc, text_bytes, text_scale, w_words, w_scales, w_bias, qn_w, k_norm, out
+):
+    nc = tc.nc
+    with ExitStack() as ctx:
+        const = ctx.enter_context(tc.tile_pool(name="const", bufs=1))
+        sb = ctx.enter_context(tc.tile_pool(name="sb", bufs=2))
+        ps = ctx.enter_context(tc.psum_pool(name="ps", bufs=1))
+        ctx.enter_context(tc.manual_schedule())
+
+        tbs, kbs = {}, {}
+
+        def load_text(b, lo, hi):
+            if b not in tbs:
+                tbs[b] = sb.tile([P, 8 * K], U8, name="tb", tag="tb", bufs=B)
+            src = text_bytes[b].rearrange("(p i) k -> p (i k)", i=8)
+            nc.sync.dma_start(out=tbs[b][:, lo:hi], in_=src[:, lo:hi])
+
+        def load_k(b):
+            kbs[b] = sb.tile([P, 2, F], BF16, name="kb", tag="kb", bufs=B)
+            nc.sync.dma_start(out=kbs[b][:], in_=k_norm[b].rearrange("(i p) k -> p i k", p=P))
+
+        load_text(0, 0, 2048)
+        sc = const.tile([P, 1, 2, 2], F32, name="sc")
+        nc.sync.dma_start(out=sc[:], in_=text_scale[0].rearrange("q (p u e) -> p q u e", u=2, e=2))
+        w_raw = const.tile([P, F], I32, name="w_raw")
+        nc.sync.dma_start(out=w_raw[:], in_=w_words[0].rearrange("p n t -> p (n t)").bitcast(I32))
+        ws_raw = const.tile([P, F], U8, name="ws_raw", align_bytes=64)
+        nc.vector.memset(ws_raw[:].bitcast(I32), 0)
+        for q in range(4):
+            nc.sync.dma_start(
+                out=ws_raw[32 * q : 32 * q + 4, :].bitcast(I32),
+                in_=w_scales[0, 4 * q : 4 * q + 4, :].bitcast(I32),
+            )
+        b16 = const.tile([P, 4], BF16, name="b16")
+        nc.sync.dma_start(out=b16[:], in_=w_bias.rearrange("(p t) -> p t", t=4))
+        g16 = const.tile([P, 4], BF16, name="g16")
+        nc.sync.dma_start(out=g16[:], in_=qn_w.rearrange("(p t) -> p t", t=4))
+        load_text(0, 2048, 4096)
+        load_k(0)
+        for b in range(1, B):
+            load_text(b, 0, 4096)
+            load_k(b)
+
+        ident = const.tile([P, P], F32, name="ident")
+        make_identity(nc, ident[:])
+        ones = const.tile([P, 1], F32, name="ones")
+        nc.gpsimd.memset(ones[:], 1.0)
+        neg_half = const.tile([P, TILES], F32, name="neg_half")
+        nc.gpsimd.memset(neg_half[:], -0.5)
+
+        w_codes = const.tile([P, F], I32, name="w_codes", align_bytes=64)
+        w_sc = const.tile([P, F], U8, name="w_sc", align_bytes=64)
+        b32 = const.tile([P, 4], F32, name="b32")
+        g32 = const.tile([P, 4], F32, name="g32")
+        bg32 = const.tile([P, 4], F32, name="bg32")
+
+        def prepare_weights():
+            nc.vector.tensor_copy(
+                out=w_codes[:].rearrange("p (t m) -> p m t", t=4),
+                in_=w_raw[:].rearrange("p (m t) -> p m t", t=4),
+            )
+            nc.vector.tensor_copy(
+                out=w_sc[:].rearrange("p (t m) -> p m t", t=4),
+                in_=ws_raw[:].rearrange("p (m t) -> p m t", t=4),
+            )
+            nc.vector.tensor_copy(out=b32[:], in_=b16[:])
+            nc.vector.tensor_copy(out=g32[:], in_=g16[:])
+            nc.vector.tensor_tensor(out=bg32[:], in0=b32[:], in1=g32[:], op=ALU.mult)
+
+        xb, tp, xg, xc, xs = {}, {}, {}, {}, {}
+        qt, y, sq, ss, rstd, rb, zg, zc, zs = {}, {}, {}, {}, {}, {}, {}, {}, {}
+        kgs, kc, ks, osb = {}, {}, {}, {}
+
+        def live(g):
+            return 0 <= g < NG
+
+        def cast(g, on_vector, tiles):
+            if not live(g):
+                return
+            if g not in xb:
+                xb[g] = sb.tile([P, TILES * K], BF16, name="xb", tag="xb", bufs=2)
+            lo, hi = tiles.start * K, tiles.stop * K
+            base = (g % 2) * TILES * K
+            src = tbs[g // 2][:, base + lo : base + hi].bitcast(F8)
+            if on_vector:
+                nc.vector.tensor_copy(out=xb[g][:, lo:hi], in_=src)
+            else:
+                nc.scalar.copy(out=xb[g][:, lo:hi], in_=src)
+
+        def turn(g, h):
+            if not live(g):
+                return
+            tp[g, h] = ps.tile([P, 2, 256], F32, name="tp", tag="tp", bufs=2)
+            words = xb[g][:].bitcast(F32)
+            for j in range(2):
+                i = 2 * h + j
+                for u in range(2):
+                    nc.tensor.transpose(
+                        tp[g, h][:, u, j * P : (j + 1) * P],
+                        words[:, i * 256 + u : (i + 1) * 256 : 2],
+                        ident[:],
+                    )
+
+        def scale_out(g, h):
+            if not live(g):
+                return
+            if h == 0:
+                xg[g] = sb.tile([P, GT * 4], BF16, name="xg", tag="xg", bufs=2, align_bytes=64)
+            nc.vector.tensor_tensor(
+                out=xg[g][:, h * 1024 : (h + 1) * 1024].rearrange("p (r u e) -> p r u e", u=2, e=2),
+                in0=tp[g, h][:].bitcast(BF16).rearrange("p u (r e) -> p r u e", e=2),
+                in1=sc[:].to_broadcast([P, 256, 2, 2]),
+                op=ALU.mult,
+            )
+
+        def quant_x(g):
+            if not live(g):
+                return
+            xc[g] = sb.tile([P, GT], U32, name="xc", tag="xc", bufs=3, align_bytes=64)
+            xs[g] = sb.tile([P, GT], U8, name="xs", tag="xs", bufs=3, align_bytes=64)
+            nc.vector.quantize_mx(out=xc[g][:].bitcast(FP8X4), scales=xs[g][:], in_=xg[g][:])
+
+        def project(g, t):
+            if not live(g):
+                return
+            qt[g, t] = ps.tile([P, GT], F32, name="q", tag="q", bufs=3)
+            cols = slice(t * P, (t + 1) * P)
+            nc.tensor.matmul_mx(
+                out=qt[g, t][:],
+                lhsT=w_codes[:, cols].bitcast(FP8X4),
+                lhsT_scale=w_sc[:, cols],
+                rhs=xc[g][:].bitcast(FP8X4),
+                rhs_scale=xs[g][:],
+                start=True,
+                stop=True,
+            )
+
+        def bias_gain_square(g, t):
+            if not live(g):
+                return
+            if t == 0:
+                y[g] = sb.tile([P, 4, GT], F32, name="y", tag="y", bufs=3)
+                sq[g] = sb.tile([P, 4, GT], F32, name="sq", tag="sq", bufs=2)
+            nc.scalar.activation(
+                out=sq[g][:, t, :], in_=qt[g, t][:], func=ACT.Square, bias=b32[:, t : t + 1]
+            )
+            nc.scalar.activation(
+                out=y[g][:, t, :],
+                in_=qt[g, t][:],
+                func=ACT.Identity,
+                bias=bg32[:, t : t + 1],
+                scale=g32[:, t : t + 1],
+            )
+
+        def sum_squares(g, t):
+            if not live(g):
+                return
+            if t == 0:
+                ss[g] = ps.tile([P, TILES, 4], F32, name="ss", tag="ss", bufs=1)
+            for j in range(TILES):
+                nc.tensor.matmul(
+                    ss[g][:, j, t : t + 1],
+                    lhsT=sq[g][:, t, j * P : (j + 1) * P],
+                    rhs=ones[:],
+                    start=True,
+                    stop=True,
+                )
+
+        def inverse_rms(g):
+            if not live(g):
+                return
+            tot = sb.tile([P, TILES], F32, name="tot", tag="tot", bufs=2)
+            nc.vector.tensor_reduce(out=tot[:], in_=ss[g][:], axis=AXIS.X, op=ALU.add)
+            ms = sb.tile([P, TILES], F32, name="ms", tag="ms", bufs=2)
+            nc.gpsimd.tensor_scalar(
+                out=ms[:], in0=tot[:], scalar1=1.0 / F, scalar2=EPS, op0=ALU.mult, op1=ALU.add
+            )
+            rstd[g] = sb.tile([P, TILES], F32, name="rstd", tag="rstd", bufs=3)
+            nc.gpsimd.tensor_tensor(out=rstd[g][:], in0=ms[:], in1=neg_half[:], op=ALU.pow)
+
+        def spread_rms(g):
+            if not live(g):
+                return
+            rb[g] = ps.tile([P, GT, 1], F32, name="rb", tag="rb", bufs=1)
+            for j in range(TILES):
+                nc.tensor.transpose(
+                    rb[g][:, j * P : (j + 1) * P, 0],
+                    rstd[g][:, j : j + 1].to_broadcast([P, P]),
+                    ident[:],
+                )
+
+        def normalise(g):
+            if not live(g):
+                return
+            zg[g] = sb.tile([P, GT * 4], BF16, name="zg", tag="zg", bufs=2, align_bytes=64)
+            nc.vector.tensor_tensor(
+                out=zg[g][:].rearrange("p (c t) -> p c t", t=4),
+                in0=y[g][:].rearrange("p t c -> p c t"),
+                in1=rb[g][:].to_broadcast([P, GT, 4]),
+                op=ALU.mult,
+            )
+
+        def quant_z(g):
+            if not live(g):
+                return
+            zc[g] = sb.tile([P, GT], U32, name="zc", tag="zc", bufs=3, align_bytes=64)
+            zs[g] = sb.tile([P, GT], U8, name="zs", tag="zs", bufs=3, align_bytes=64)
+            nc.vector.quantize_mx(out=zc[g][:].bitcast(FP8X4), scales=zs[g][:], in_=zg[g][:])
+
+        def keys(b):
+            if not 0 <= b < B:
+                return
+            kt = ps.tile([P, 2, 256], F32, name="kt", tag="o", bufs=1)
+            words = kbs[b][:].rearrange("p i k -> p (i k)").bitcast(F32)
+            for i in range(2):
+                for u in range(2):
+                    nc.tensor.transpose(
+                        kt[:, u, i * P : (i + 1) * P],
+                        words[:, i * 256 + u : (i + 1) * 256 : 2],
+                        ident[:],
+                    )
+            kg = sb.tile([P, S * 4], BF16, name="kg", tag="kg", bufs=2, align_bytes=64)
+            nc.scalar.copy(
+                out=kg[:].bitcast(F32).rearrange("p (r u) -> p r u", u=2),
+                in_=kt[:].rearrange("p u r -> p r u"),
+            )
+            kgs[b] = kg
+
+        def quant_k(b):
+            if not 0 <= b < B:
+                return
+            kc[b] = sb.tile([P, S], U32, name="kc", tag="kc", bufs=3, align_bytes=64)
+            ks[b] = sb.tile([P, S], U8, name="ks", tag="ks", bufs=3, align_bytes=64)
+            nc.vector.quantize_mx(out=kc[b][:].bitcast(FP8X4), scales=ks[b][:], in_=kgs[b][:])
+
+        def attend(g, h):
+            if not live(g):
+                return
+            b = g // 2
+            o = ps.tile([P, 2, S], F32, name="o", tag="o", bufs=1)
+            for j in range(2):
+                cols = slice((2 * h + j) * P, (2 * h + j + 1) * P)
+                nc.tensor.matmul_mx(
+                    out=o[:, j, :],
+                    lhsT=zc[g][:, cols].bitcast(FP8X4),
+                    lhsT_scale=zs[g][:, cols],
+                    rhs=kc[b][:].bitcast(FP8X4),
+                    rhs_scale=ks[b][:],
+                    start=True,
+                    stop=True,
+                )
+            if h == 0:
+                osb[g] = sb.tile([P, TILES, S], F32, name="osb", tag="osb", bufs=3)
+            nc.scalar.activation(
+                out=osb[g][:, 2 * h : 2 * h + 2, :], in_=o[:], func=ACT.Copy, scale=F**-0.5
+            )
+            if h == 1:
+                i0 = (g % 2) * TILES
+                dst = out[b].rearrange("(p i) s -> p i s", i=8)
+                nc.sync.dma_start(out=dst[:, i0 : i0 + TILES, :], in_=osb[g][:])
+
+        for s in range(-4, NG + 4):
+            normalise(s - 2)
+            sum_squares(s - 1, 3)
+            inverse_rms(s - 1)
+            bias_gain_square(s, 0)
+            project(s, 2)
+            attend(s - 3, 0)
+            scale_out(s + 2, 0)
+            sum_squares(s, 0)
+            quant_z(s - 2)
+            bias_gain_square(s, 1)
+            project(s, 3)
+            attend(s - 3, 1)
+            turn(s + 3, 0)
+            scale_out(s + 2, 1)
+            sum_squares(s, 1)
+            bias_gain_square(s, 2)
+            project(s + 1, 0)
+            if s % 2 == 0:
+                keys(s // 2)
+            if s == -3:
+                prepare_weights()
+            cast(s + 4, True, slice(0, 2))
+            turn(s + 3, 1)
+            quant_x(s + 2)
+            sum_squares(s, 2)
+            spread_rms(s - 1)
+            if s % 2 == 0:
+                quant_k(s // 2)
+            bias_gain_square(s, 3)
+            project(s + 1, 1)
+            cast(s + 4, False, slice(2, 4))

@@ -70,10 +70,8 @@ def tile_crossattention_pb_t_w8_kernel(
 
         ident = const.tile([P, P], F32, name="ident")
         make_identity(nc, ident[:])
-        ones = const.tile([P, 1], F32, name="ones")
-        nc.gpsimd.memset(ones[:], 1.0)
-        neg_half = const.tile([P, TILES], F32, name="neg_half")
-        nc.gpsimd.memset(neg_half[:], -0.5)
+        eps = const.tile([P, 1], F32, name="eps")
+        nc.gpsimd.memset(eps[:], EPS)
 
         w_codes = const.tile([P, F], I32, name="w_codes", align_bytes=64)
         w_sc = const.tile([P, F], U8, name="w_sc", align_bytes=64)
@@ -95,24 +93,26 @@ def tile_crossattention_pb_t_w8_kernel(
             nc.vector.tensor_tensor(out=bg32[:], in0=b32[:], in1=g32[:], op=ALU.mult)
 
         xb, tp, xg, xc, xs = {}, {}, {}, {}, {}
-        qt, y, sq, ss, rstd, rb, zg, zc, zs = {}, {}, {}, {}, {}, {}, {}, {}, {}
-        kgs, kc, ks, osb = {}, {}, {}, {}
+        qt, y, sq, ss, tot, rstd, rb, zg, zc, zs = {}, {}, {}, {}, {}, {}, {}, {}, {}, {}
+        kts, kgs, kc, ks, ot, osb = {}, {}, {}, {}, {}, {}
 
         def live(g):
             return 0 <= g < NG
 
-        def cast(g, on_vector, tiles):
+        def cast(g, engine, i, n):
             if not live(g):
                 return
             if g not in xb:
                 xb[g] = sb.tile([P, TILES * K], BF16, name="xb", tag="xb", bufs=2)
-            lo, hi = tiles.start * K, tiles.stop * K
+            lo, hi = i * K, (i + n) * K
             base = (g % 2) * TILES * K
             src = tbs[g // 2][:, base + lo : base + hi].bitcast(F8)
-            if on_vector:
+            if engine == "v":
                 nc.vector.tensor_copy(out=xb[g][:, lo:hi], in_=src)
-            else:
+            elif engine == "s":
                 nc.scalar.copy(out=xb[g][:, lo:hi], in_=src)
+            else:
+                nc.gpsimd.tensor_copy(out=xb[g][:, lo:hi], in_=src)
 
         def turn(g, h):
             if not live(g):
@@ -166,7 +166,7 @@ def tile_crossattention_pb_t_w8_kernel(
             if not live(g):
                 return
             if t == 0:
-                y[g] = sb.tile([P, 4, GT], F32, name="y", tag="y", bufs=3)
+                y[g] = sb.tile([P, 4, GT], F32, name="y", tag="y", bufs=2)
                 sq[g] = sb.tile([P, 4, GT], F32, name="sq", tag="sq", bufs=2)
             nc.scalar.activation(
                 out=sq[g][:, t, :], in_=qt[g, t][:], func=ACT.Square, bias=b32[:, t : t + 1]
@@ -179,36 +179,39 @@ def tile_crossattention_pb_t_w8_kernel(
                 scale=g32[:, t : t + 1],
             )
 
-        def sum_squares(g, t):
+        def sum_squares(g):
             if not live(g):
                 return
-            if t == 0:
-                ss[g] = ps.tile([P, TILES, 4], F32, name="ss", tag="ss", bufs=1)
+            ss[g] = ps.tile([P, TILES, P], F32, name="ss", tag="ss", bufs=1)
             for j in range(TILES):
-                nc.tensor.matmul(
-                    ss[g][:, j, t : t + 1],
-                    lhsT=sq[g][:, t, j * P : (j + 1) * P],
-                    rhs=ones[:],
-                    start=True,
-                    stop=True,
-                )
+                for t in range(4):
+                    nc.tensor.matmul(
+                        ss[g][:, j, :],
+                        lhsT=sq[g][:, t, j * P : (j + 1) * P],
+                        rhs=ident[:],
+                        start=(t == 0),
+                        stop=(t == 3),
+                        is_transpose=True,
+                    )
+
+        def total(g):
+            if not live(g):
+                return
+            tot[g] = sb.tile([P, TILES], F32, name="tot", tag="tot", bufs=2)
+            nc.vector.tensor_reduce(out=tot[g][:], in_=ss[g][:], axis=AXIS.X, op=ALU.add)
 
         def inverse_rms(g):
             if not live(g):
                 return
-            tot = sb.tile([P, TILES], F32, name="tot", tag="tot", bufs=2)
-            nc.vector.tensor_reduce(out=tot[:], in_=ss[g][:], axis=AXIS.X, op=ALU.add)
-            ms = sb.tile([P, TILES], F32, name="ms", tag="ms", bufs=2)
-            nc.gpsimd.tensor_scalar(
-                out=ms[:], in0=tot[:], scalar1=1.0 / F, scalar2=EPS, op0=ALU.mult, op1=ALU.add
+            rstd[g] = sb.tile([P, TILES], F32, name="rstd", tag="rstd", bufs=2)
+            nc.scalar.activation(
+                out=rstd[g][:], in_=tot[g][:], func=ACT.Abs_reciprocal_sqrt, bias=eps[:], scale=1.0 / F
             )
-            rstd[g] = sb.tile([P, TILES], F32, name="rstd", tag="rstd", bufs=3)
-            nc.gpsimd.tensor_tensor(out=rstd[g][:], in0=ms[:], in1=neg_half[:], op=ALU.pow)
 
         def spread_rms(g):
             if not live(g):
                 return
-            rb[g] = ps.tile([P, GT, 1], F32, name="rb", tag="rb", bufs=1)
+            rb[g] = ps.tile([P, GT, 1], F32, name="rb", tag="ss", bufs=1)
             for j in range(TILES):
                 nc.tensor.transpose(
                     rb[g][:, j * P : (j + 1) * P, 0],
@@ -237,7 +240,7 @@ def tile_crossattention_pb_t_w8_kernel(
         def keys(b):
             if not 0 <= b < B:
                 return
-            kt = ps.tile([P, 2, 256], F32, name="kt", tag="o", bufs=1)
+            kt = ps.tile([P, 2, 256], F32, name="kt", tag="o", bufs=2)
             words = kbs[b][:].rearrange("p i k -> p (i k)").bitcast(F32)
             for i in range(2):
                 for u in range(2):
@@ -246,12 +249,16 @@ def tile_crossattention_pb_t_w8_kernel(
                         words[:, i * 256 + u : (i + 1) * 256 : 2],
                         ident[:],
                     )
-            kg = sb.tile([P, S * 4], BF16, name="kg", tag="kg", bufs=2, align_bytes=64)
+            kts[b] = kt
+
+        def keys_out(b):
+            if not 0 <= b < B:
+                return
+            kgs[b] = sb.tile([P, S * 4], BF16, name="kg", tag="kg", bufs=2, align_bytes=64)
             nc.scalar.copy(
-                out=kg[:].bitcast(F32).rearrange("p (r u) -> p r u", u=2),
-                in_=kt[:].rearrange("p u r -> p r u"),
+                out=kgs[b][:].bitcast(F32).rearrange("p (r u) -> p r u", u=2),
+                in_=kts[b][:].rearrange("p u r -> p r u"),
             )
-            kgs[b] = kg
 
         def quant_k(b):
             if not 0 <= b < B:
@@ -260,15 +267,15 @@ def tile_crossattention_pb_t_w8_kernel(
             ks[b] = sb.tile([P, S], U8, name="ks", tag="ks", bufs=3, align_bytes=64)
             nc.vector.quantize_mx(out=kc[b][:].bitcast(FP8X4), scales=ks[b][:], in_=kgs[b][:])
 
-        def attend(g, h):
+        def attend_mm(g, h):
             if not live(g):
                 return
             b = g // 2
-            o = ps.tile([P, 2, S], F32, name="o", tag="o", bufs=1)
+            ot[g, h] = ps.tile([P, 2, S], F32, name="o", tag="o", bufs=2)
             for j in range(2):
                 cols = slice((2 * h + j) * P, (2 * h + j + 1) * P)
                 nc.tensor.matmul_mx(
-                    out=o[:, j, :],
+                    out=ot[g, h][:, j, :],
                     lhsT=zc[g][:, cols].bitcast(FP8X4),
                     lhsT_scale=zs[g][:, cols],
                     rhs=kc[b][:].bitcast(FP8X4),
@@ -276,45 +283,57 @@ def tile_crossattention_pb_t_w8_kernel(
                     start=True,
                     stop=True,
                 )
+
+        def attend_out(g, h):
+            if not live(g):
+                return
             if h == 0:
                 osb[g] = sb.tile([P, TILES, S], F32, name="osb", tag="osb", bufs=3)
             nc.scalar.activation(
-                out=osb[g][:, 2 * h : 2 * h + 2, :], in_=o[:], func=ACT.Copy, scale=F**-0.5
+                out=osb[g][:, 2 * h : 2 * h + 2, :], in_=ot[g, h][:], func=ACT.Copy, scale=F**-0.5
             )
             if h == 1:
                 i0 = (g % 2) * TILES
-                dst = out[b].rearrange("(p i) s -> p i s", i=8)
+                dst = out[g // 2].rearrange("(p i) s -> p i s", i=8)
                 nc.sync.dma_start(out=dst[:, i0 : i0 + TILES, :], in_=osb[g][:])
 
-        for s in range(-4, NG + 4):
-            normalise(s - 2)
-            sum_squares(s - 1, 3)
-            inverse_rms(s - 1)
-            bias_gain_square(s, 0)
+        for s in range(-4, NG + 3):
             project(s, 2)
-            attend(s - 3, 0)
-            scale_out(s + 2, 0)
-            sum_squares(s, 0)
+            sum_squares(s - 1)
             quant_z(s - 2)
-            bias_gain_square(s, 1)
+            bias_gain_square(s, 0)
             project(s, 3)
-            attend(s - 3, 1)
+            scale_out(s + 2, 0)
+            if s % 2 == 1:
+                quant_k(s // 2)
+            total(s - 1)
+            attend_mm(s - 2, 0)
             turn(s + 3, 0)
+            bias_gain_square(s, 1)
+            inverse_rms(s - 1)
+            attend_out(s - 2, 0)
+            spread_rms(s - 1)
             scale_out(s + 2, 1)
-            sum_squares(s, 1)
             bias_gain_square(s, 2)
+            attend_mm(s - 2, 1)
+            attend_out(s - 2, 1)
             project(s + 1, 0)
+            turn(s + 3, 1)
             if s % 2 == 0:
                 keys(s // 2)
+            normalise(s - 1)
             if s == -3:
                 prepare_weights()
-            cast(s + 4, True, slice(0, 2))
-            turn(s + 3, 1)
-            quant_x(s + 2)
-            sum_squares(s, 2)
-            spread_rms(s - 1)
-            if s % 2 == 0:
-                quant_k(s // 2)
             bias_gain_square(s, 3)
             project(s + 1, 1)
-            cast(s + 4, False, slice(2, 4))
+            if s < -2:
+                cast(s + 4, "v", 0, 2)
+                cast(s + 4, "s", 2, 2)
+            else:
+                cast(s + 4, "g", 0, 1)
+                cast(s + 4, "g", 1, 1)
+                cast(s + 4, "v", 2, 1)
+                cast(s + 4, "s", 3, 1)
+            quant_x(s + 2)
+            if s % 2 == 0:
+                keys_out(s // 2)

@@ -150,7 +150,7 @@ def tile_crossattention_pb_t_w8_kernel(
         def project(g, t):
             if not live(g):
                 return
-            qt[g, t] = ps.tile([P, GT], F32, name="q", tag="q", bufs=3)
+            qt[g, t] = ps.tile([P, GT], F32, name="q", tag="q", bufs=4)
             cols = slice(t * P, (t + 1) * P)
             nc.tensor.matmul_mx(
                 out=qt[g, t][:],
@@ -162,15 +162,20 @@ def tile_crossattention_pb_t_w8_kernel(
                 stop=True,
             )
 
-        def bias_gain_square(g, t):
+        def squares(g, t):
             if not live(g):
                 return
             if t == 0:
-                y[g] = sb.tile([P, 4, GT], F32, name="y", tag="y", bufs=2)
                 sq[g] = sb.tile([P, 4, GT], F32, name="sq", tag="sq", bufs=2)
             nc.scalar.activation(
                 out=sq[g][:, t, :], in_=qt[g, t][:], func=ACT.Square, bias=b32[:, t : t + 1]
             )
+
+        def gained(g, t):
+            if not live(g):
+                return
+            if t == 0:
+                y[g] = sb.tile([P, 4, GT], F32, name="y", tag="y", bufs=2)
             nc.scalar.activation(
                 out=y[g][:, t, :],
                 in_=qt[g, t][:],
@@ -211,10 +216,10 @@ def tile_crossattention_pb_t_w8_kernel(
         def spread_rms(g):
             if not live(g):
                 return
-            rb[g] = ps.tile([P, GT, 1], F32, name="rb", tag="ss", bufs=1)
+            rb[g] = ps.tile([P, GT // 4, 1, 4], F32, name="rb", tag="rb", bufs=1)
             for j in range(TILES):
                 nc.tensor.transpose(
-                    rb[g][:, j * P : (j + 1) * P, 0],
+                    rb[g][:].rearrange("p c o i -> p (c o i)")[:, j * P : (j + 1) * P],
                     rstd[g][:, j : j + 1].to_broadcast([P, P]),
                     ident[:],
                 )
@@ -224,9 +229,9 @@ def tile_crossattention_pb_t_w8_kernel(
                 return
             zg[g] = sb.tile([P, GT * 4], BF16, name="zg", tag="zg", bufs=2, align_bytes=64)
             nc.vector.tensor_tensor(
-                out=zg[g][:].rearrange("p (c t) -> p c t", t=4),
-                in0=y[g][:].rearrange("p t c -> p c t"),
-                in1=rb[g][:].to_broadcast([P, GT, 4]),
+                out=zg[g][:].rearrange("p (c i t) -> p c t i", i=4, t=4),
+                in0=y[g][:].rearrange("p t (c i) -> p c t i", i=4),
+                in1=rb[g][:].to_broadcast([P, GT // 4, 4, 4]),
                 op=ALU.mult,
             )
 
@@ -240,7 +245,7 @@ def tile_crossattention_pb_t_w8_kernel(
         def keys(b):
             if not 0 <= b < B:
                 return
-            kt = ps.tile([P, 2, 256], F32, name="kt", tag="o", bufs=2)
+            kt = ps.tile([P, 2, 256], F32, name="kt", tag="q", bufs=4)
             words = kbs[b][:].rearrange("p i k -> p (i k)").bitcast(F32)
             for i in range(2):
                 for u in range(2):
@@ -271,7 +276,7 @@ def tile_crossattention_pb_t_w8_kernel(
             if not live(g):
                 return
             b = g // 2
-            ot[g, h] = ps.tile([P, 2, S], F32, name="o", tag="o", bufs=2)
+            ot[g, h] = ps.tile([P, 2, S], F32, name="o", tag="q", bufs=4)
             for j in range(2):
                 cols = slice((2 * h + j) * P, (2 * h + j + 1) * P)
                 nc.tensor.matmul_mx(
@@ -289,51 +294,63 @@ def tile_crossattention_pb_t_w8_kernel(
                 return
             if h == 0:
                 osb[g] = sb.tile([P, TILES, S], F32, name="osb", tag="osb", bufs=3)
-            nc.scalar.activation(
-                out=osb[g][:, 2 * h : 2 * h + 2, :], in_=ot[g, h][:], func=ACT.Copy, scale=F**-0.5
-            )
-            if h == 1:
-                i0 = (g % 2) * TILES
-                dst = out[g // 2].rearrange("(p i) s -> p i s", i=8)
+            rows = slice(2 * h, 2 * h + 2)
+            if g == NG - 1 and h == 1:
+                nc.vector.tensor_scalar(
+                    out=osb[g][:, rows, :], in0=ot[g, h][:], scalar1=F**-0.5, scalar2=None, op0=ALU.mult
+                )
+            else:
+                nc.scalar.activation(
+                    out=osb[g][:, rows, :], in_=ot[g, h][:], func=ACT.Copy, scale=F**-0.5
+                )
+            i0 = (g % 2) * TILES
+            dst = out[g // 2].rearrange("(p i) s -> p i s", i=8)
+            if g == NG - 1:
+                nc.sync.dma_start(out=dst[:, i0 + 2 * h : i0 + 2 * h + 2, :], in_=osb[g][:, rows, :])
+            elif h == 1:
                 nc.sync.dma_start(out=dst[:, i0 : i0 + TILES, :], in_=osb[g][:])
 
         for s in range(-4, NG + 3):
-            project(s, 2)
-            sum_squares(s - 1)
-            quant_z(s - 2)
-            bias_gain_square(s, 0)
-            project(s, 3)
             scale_out(s + 2, 0)
+            project(s, 1)
+            squares(s, 0)
+            gained(s, 0)
+            squares(s, 1)
+            project(s, 2)
+            attend_mm(s - 2, 0)
+            total(s - 1)
+            project(s, 3)
+            inverse_rms(s - 1)
+            spread_rms(s - 1)
+            attend_out(s - 2, 0)
+            squares(s, 2)
+            squares(s, 3)
+            attend_mm(s - 2, 1)
+            scale_out(s + 2, 1)
+            project(s + 1, 0)
+            gained(s, 1)
+            turn(s + 3, 0)
+            if s == -3:
+                prepare_weights()
             if s % 2 == 1:
                 quant_k(s // 2)
-            total(s - 1)
-            attend_mm(s - 2, 0)
-            turn(s + 3, 0)
-            bias_gain_square(s, 1)
-            inverse_rms(s - 1)
-            attend_out(s - 2, 0)
-            spread_rms(s - 1)
-            scale_out(s + 2, 1)
-            bias_gain_square(s, 2)
-            attend_mm(s - 2, 1)
-            attend_out(s - 2, 1)
-            project(s + 1, 0)
             turn(s + 3, 1)
+            if s == -4:
+                cast(s + 4, "v", 0, 2)
+                cast(s + 4, "s", 2, 2)
+            elif s == -3:
+                cast(s + 4, "s", 0, 4)
+            else:
+                for i in range(TILES):
+                    cast(s + 4, "g", i, 1)
             if s % 2 == 0:
                 keys(s // 2)
             normalise(s - 1)
-            if s == -3:
-                prepare_weights()
-            bias_gain_square(s, 3)
-            project(s + 1, 1)
-            if s < -2:
-                cast(s + 4, "v", 0, 2)
-                cast(s + 4, "s", 2, 2)
-            else:
-                cast(s + 4, "g", 0, 1)
-                cast(s + 4, "g", 1, 1)
-                cast(s + 4, "v", 2, 1)
-                cast(s + 4, "s", 3, 1)
-            quant_x(s + 2)
+            attend_out(s - 2, 1)
+            gained(s, 2)
+            gained(s, 3)
             if s % 2 == 0:
                 keys_out(s // 2)
+            sum_squares(s)
+            quant_x(s + 2)
+            quant_z(s - 1)

@@ -19,9 +19,12 @@ ACT = mybir.ActivationFunctionType
 AXIS = mybir.AxisListType
 
 P = 128
-GT = 512
-NG = B * T // GT
-TILES = GT // P
+PT = 2 * P
+NP = B * T // PT
+PPB = T // PT
+ROWS = T // P
+GROUPS = [[0]] + [[i, i + 1] for i in range(1, NP - 1, 2)] + [[NP - 1]]
+NG = len(GROUPS)
 
 
 def tile_crossattention_pb_t_w8_kernel(
@@ -38,19 +41,20 @@ def tile_crossattention_pb_t_w8_kernel(
 
         def load_text(b, lo, hi):
             if b not in tbs:
-                tbs[b] = sb.tile([P, 8 * K], U8, name="tb", tag="tb", bufs=B)
-            src = text_bytes[b].rearrange("(p i) k -> p (i k)", i=8)
+                tbs[b] = sb.tile([P, ROWS * K], U8, name="tb", tag="tb", bufs=B)
+            src = text_bytes[b].rearrange("(p i) k -> p (i k)", i=ROWS)
             nc.sync.dma_start(out=tbs[b][:, lo:hi], in_=src[:, lo:hi])
 
-        def load_k(b):
+        def load_keys(b):
             kbs[b] = sb.tile([P, 2, F], BF16, name="kb", tag="kb", bufs=B)
             nc.sync.dma_start(out=kbs[b][:], in_=k_norm[b].rearrange("(i p) k -> p i k", p=P))
 
-        load_text(0, 0, 2048)
+        load_text(0, 0, 2 * K)
         sc = const.tile([P, 1, 2, 2], F32, name="sc")
         nc.sync.dma_start(out=sc[:], in_=text_scale[0].rearrange("q (p u e) -> p q u e", u=2, e=2))
         w_raw = const.tile([P, F], I32, name="w_raw")
         nc.sync.dma_start(out=w_raw[:], in_=w_words[0].rearrange("p n t -> p (n t)").bitcast(I32))
+        load_text(0, 2 * K, ROWS * K)
         ws_raw = const.tile([P, F], U8, name="ws_raw", align_bytes=64)
         nc.vector.memset(ws_raw[:].bitcast(I32), 0)
         for q in range(4):
@@ -62,11 +66,10 @@ def tile_crossattention_pb_t_w8_kernel(
         nc.sync.dma_start(out=b16[:], in_=w_bias.rearrange("(p t) -> p t", t=4))
         g16 = const.tile([P, 4], BF16, name="g16")
         nc.sync.dma_start(out=g16[:], in_=qn_w.rearrange("(p t) -> p t", t=4))
-        load_text(0, 2048, 4096)
-        load_k(0)
+        load_keys(0)
         for b in range(1, B):
-            load_text(b, 0, 4096)
-            load_k(b)
+            load_text(b, 0, ROWS * K)
+            load_keys(b)
 
         ident = const.tile([P, P], F32, name="ident")
         make_identity(nc, ident[:])
@@ -96,61 +99,64 @@ def tile_crossattention_pb_t_w8_kernel(
         qt, y, sq, ss, tot, rstd, rb, zg, zc, zs = {}, {}, {}, {}, {}, {}, {}, {}, {}, {}
         kts, kgs, kc, ks, ot, osb = {}, {}, {}, {}, {}, {}
 
-        def live(g):
-            return 0 <= g < NG
+        def has(g, h=0):
+            return 0 <= g < NG and h < len(GROUPS[g])
 
-        def cast(g, engine, i, n):
-            if not live(g):
+        def width(g):
+            return len(GROUPS[g]) * PT
+
+        def cast(g, h, engines):
+            if not has(g, h):
                 return
-            if g not in xb:
-                xb[g] = sb.tile([P, TILES * K], BF16, name="xb", tag="xb", bufs=2)
-            lo, hi = i * K, (i + n) * K
-            base = (g % 2) * TILES * K
-            src = tbs[g // 2][:, base + lo : base + hi].bitcast(F8)
-            if engine == "v":
-                nc.vector.tensor_copy(out=xb[g][:, lo:hi], in_=src)
-            elif engine == "s":
-                nc.scalar.copy(out=xb[g][:, lo:hi], in_=src)
-            else:
-                nc.gpsimd.tensor_copy(out=xb[g][:, lo:hi], in_=src)
+            xb[g, h] = sb.tile([P, 2 * K], BF16, name="xb", tag="xb", bufs=4)
+            pair = GROUPS[g][h]
+            for j in range(2):
+                base = ((pair % PPB) * 2 + j) * K
+                src = tbs[pair // PPB][:, base : base + K].bitcast(F8)
+                dst = xb[g, h][:, j * K : (j + 1) * K]
+                if engines[j] == "v":
+                    nc.vector.tensor_copy(out=dst, in_=src)
+                elif engines[j] == "s":
+                    nc.scalar.copy(out=dst, in_=src)
+                else:
+                    nc.gpsimd.tensor_copy(out=dst, in_=src)
 
         def turn(g, h):
-            if not live(g):
+            if not has(g, h):
                 return
-            tp[g, h] = ps.tile([P, 2, 256], F32, name="tp", tag="tp", bufs=2)
-            words = xb[g][:].bitcast(F32)
+            tp[g, h] = ps.tile([P, 2, PT], F32, name="tp", tag="tp", bufs=2)
+            words = xb[g, h][:].bitcast(F32)
             for j in range(2):
-                i = 2 * h + j
                 for u in range(2):
                     nc.tensor.transpose(
                         tp[g, h][:, u, j * P : (j + 1) * P],
-                        words[:, i * 256 + u : (i + 1) * 256 : 2],
+                        words[:, j * 256 + u : (j + 1) * 256 : 2],
                         ident[:],
                     )
 
         def scale_out(g, h):
-            if not live(g):
+            if not has(g, h):
                 return
             if h == 0:
-                xg[g] = sb.tile([P, GT * 4], BF16, name="xg", tag="xg", bufs=2, align_bytes=64)
+                xg[g] = sb.tile([P, width(g) * 4], BF16, name="xg", tag="xg", bufs=2, align_bytes=64)
             nc.vector.tensor_tensor(
-                out=xg[g][:, h * 1024 : (h + 1) * 1024].rearrange("p (r u e) -> p r u e", u=2, e=2),
+                out=xg[g][:, h * PT * 4 : (h + 1) * PT * 4].rearrange("p (r u e) -> p r u e", u=2, e=2),
                 in0=tp[g, h][:].bitcast(BF16).rearrange("p u (r e) -> p r u e", e=2),
-                in1=sc[:].to_broadcast([P, 256, 2, 2]),
+                in1=sc[:].to_broadcast([P, PT, 2, 2]),
                 op=ALU.mult,
             )
 
         def quant_x(g):
-            if not live(g):
+            if not has(g):
                 return
-            xc[g] = sb.tile([P, GT], U32, name="xc", tag="xc", bufs=3, align_bytes=64)
-            xs[g] = sb.tile([P, GT], U8, name="xs", tag="xs", bufs=3, align_bytes=64)
+            xc[g] = sb.tile([P, width(g)], U32, name="xc", tag="xc", bufs=3, align_bytes=64)
+            xs[g] = sb.tile([P, width(g)], U8, name="xs", tag="xs", bufs=3, align_bytes=64)
             nc.vector.quantize_mx(out=xc[g][:].bitcast(FP8X4), scales=xs[g][:], in_=xg[g][:])
 
         def project(g, t):
-            if not live(g):
+            if not has(g) or (g, t) in qt:
                 return
-            qt[g, t] = ps.tile([P, GT], F32, name="q", tag="q", bufs=4)
+            qt[g, t] = ps.tile([P, width(g)], F32, name="q", tag="q", bufs=4)
             cols = slice(t * P, (t + 1) * P)
             nc.tensor.matmul_mx(
                 out=qt[g, t][:],
@@ -163,19 +169,19 @@ def tile_crossattention_pb_t_w8_kernel(
             )
 
         def squares(g, t):
-            if not live(g):
+            if not has(g):
                 return
             if t == 0:
-                sq[g] = sb.tile([P, 4, GT], F32, name="sq", tag="sq", bufs=2)
+                sq[g] = sb.tile([P, 4, width(g)], F32, name="sq", tag="sq", bufs=2)
             nc.scalar.activation(
                 out=sq[g][:, t, :], in_=qt[g, t][:], func=ACT.Square, bias=b32[:, t : t + 1]
             )
 
         def gained(g, t):
-            if not live(g):
+            if not has(g):
                 return
             if t == 0:
-                y[g] = sb.tile([P, 4, GT], F32, name="y", tag="y", bufs=2)
+                y[g] = sb.tile([P, 4, width(g)], F32, name="y", tag="y", bufs=2)
             nc.scalar.activation(
                 out=y[g][:, t, :],
                 in_=qt[g, t][:],
@@ -185,10 +191,11 @@ def tile_crossattention_pb_t_w8_kernel(
             )
 
         def sum_squares(g):
-            if not live(g):
+            if not has(g):
                 return
-            ss[g] = ps.tile([P, TILES, P], F32, name="ss", tag="ss", bufs=1)
-            for j in range(TILES):
+            tiles = width(g) // P
+            ss[g] = ps.tile([P, tiles, P], F32, name="ss", tag="ss", bufs=1)
+            for j in range(tiles):
                 for t in range(4):
                     nc.tensor.matmul(
                         ss[g][:, j, :],
@@ -200,61 +207,59 @@ def tile_crossattention_pb_t_w8_kernel(
                     )
 
         def total(g):
-            if not live(g):
+            if not has(g):
                 return
-            tot[g] = sb.tile([P, TILES], F32, name="tot", tag="tot", bufs=2)
+            tot[g] = sb.tile([P, width(g) // P], F32, name="tot", tag="tot", bufs=2)
             nc.vector.tensor_reduce(out=tot[g][:], in_=ss[g][:], axis=AXIS.X, op=ALU.add)
 
         def inverse_rms(g):
-            if not live(g):
+            if not has(g):
                 return
-            rstd[g] = sb.tile([P, TILES], F32, name="rstd", tag="rstd", bufs=2)
+            rstd[g] = sb.tile([P, width(g) // P], F32, name="rstd", tag="rstd", bufs=2)
             nc.scalar.activation(
                 out=rstd[g][:], in_=tot[g][:], func=ACT.Abs_reciprocal_sqrt, bias=eps[:], scale=1.0 / F
             )
 
         def spread_rms(g):
-            if not live(g):
+            if not has(g):
                 return
-            rb[g] = ps.tile([P, GT // 4, 1, 4], F32, name="rb", tag="rb", bufs=1)
-            for j in range(TILES):
+            rb[g] = ps.tile([P, width(g) // 4, 1, 4], F32, name="rb", tag="rb", bufs=1)
+            row = rb[g][:].rearrange("p c o i -> p (c o i)")
+            for j in range(width(g) // P):
                 nc.tensor.transpose(
-                    rb[g][:].rearrange("p c o i -> p (c o i)")[:, j * P : (j + 1) * P],
-                    rstd[g][:, j : j + 1].to_broadcast([P, P]),
-                    ident[:],
+                    row[:, j * P : (j + 1) * P], rstd[g][:, j : j + 1].to_broadcast([P, P]), ident[:]
                 )
 
         def normalise(g):
-            if not live(g):
+            if not has(g):
                 return
-            zg[g] = sb.tile([P, GT * 4], BF16, name="zg", tag="zg", bufs=2, align_bytes=64)
+            zg[g] = sb.tile([P, width(g) * 4], BF16, name="zg", tag="zg", bufs=2, align_bytes=64)
             nc.vector.tensor_tensor(
                 out=zg[g][:].rearrange("p (c i t) -> p c t i", i=4, t=4),
                 in0=y[g][:].rearrange("p t (c i) -> p c t i", i=4),
-                in1=rb[g][:].to_broadcast([P, GT // 4, 4, 4]),
+                in1=rb[g][:].to_broadcast([P, width(g) // 4, 4, 4]),
                 op=ALU.mult,
             )
 
         def quant_z(g):
-            if not live(g):
+            if not has(g):
                 return
-            zc[g] = sb.tile([P, GT], U32, name="zc", tag="zc", bufs=3, align_bytes=64)
-            zs[g] = sb.tile([P, GT], U8, name="zs", tag="zs", bufs=3, align_bytes=64)
+            zc[g] = sb.tile([P, width(g)], U32, name="zc", tag="zc", bufs=3, align_bytes=64)
+            zs[g] = sb.tile([P, width(g)], U8, name="zs", tag="zs", bufs=3, align_bytes=64)
             nc.vector.quantize_mx(out=zc[g][:].bitcast(FP8X4), scales=zs[g][:], in_=zg[g][:])
 
         def keys(b):
             if not 0 <= b < B:
                 return
-            kt = ps.tile([P, 2, 256], F32, name="kt", tag="q", bufs=4)
+            kts[b] = ps.tile([P, 2, S], F32, name="kt", tag="q", bufs=4)
             words = kbs[b][:].rearrange("p i k -> p (i k)").bitcast(F32)
             for i in range(2):
                 for u in range(2):
                     nc.tensor.transpose(
-                        kt[:, u, i * P : (i + 1) * P],
+                        kts[b][:, u, i * P : (i + 1) * P],
                         words[:, i * 256 + u : (i + 1) * 256 : 2],
                         ident[:],
                     )
-            kts[b] = kt
 
         def keys_out(b):
             if not 0 <= b < B:
@@ -273,9 +278,9 @@ def tile_crossattention_pb_t_w8_kernel(
             nc.vector.quantize_mx(out=kc[b][:].bitcast(FP8X4), scales=ks[b][:], in_=kgs[b][:])
 
         def attend_mm(g, h):
-            if not live(g):
+            if not has(g, h):
                 return
-            b = g // 2
+            b = GROUPS[g][h] // PPB
             ot[g, h] = ps.tile([P, 2, S], F32, name="o", tag="q", bufs=4)
             for j in range(2):
                 cols = slice((2 * h + j) * P, (2 * h + j + 1) * P)
@@ -290,67 +295,59 @@ def tile_crossattention_pb_t_w8_kernel(
                 )
 
         def attend_out(g, h):
-            if not live(g):
+            if not has(g, h):
                 return
-            if h == 0:
-                osb[g] = sb.tile([P, TILES, S], F32, name="osb", tag="osb", bufs=3)
-            rows = slice(2 * h, 2 * h + 2)
-            if g == NG - 1 and h == 1:
-                nc.vector.tensor_scalar(
-                    out=osb[g][:, rows, :], in0=ot[g, h][:], scalar1=F**-0.5, scalar2=None, op0=ALU.mult
-                )
-            else:
-                nc.scalar.activation(
-                    out=osb[g][:, rows, :], in_=ot[g, h][:], func=ACT.Copy, scale=F**-0.5
-                )
-            i0 = (g % 2) * TILES
-            dst = out[g // 2].rearrange("(p i) s -> p i s", i=8)
-            if g == NG - 1:
-                nc.sync.dma_start(out=dst[:, i0 + 2 * h : i0 + 2 * h + 2, :], in_=osb[g][:, rows, :])
-            elif h == 1:
-                nc.sync.dma_start(out=dst[:, i0 : i0 + TILES, :], in_=osb[g][:])
+            pair = GROUPS[g][h]
+            osb[g, h] = sb.tile([P, 2, S], F32, name="osb", tag="osb", bufs=6)
+            nc.scalar.activation(out=osb[g, h][:], in_=ot[g, h][:], func=ACT.Copy, scale=F**-0.5)
+            i0 = (pair % PPB) * 2
+            dst = out[pair // PPB].rearrange("(p i) s -> p i s", i=ROWS)
+            nc.sync.dma_start(out=dst[:, i0 : i0 + 2, :], in_=osb[g, h][:])
 
         for s in range(-4, NG + 3):
-            scale_out(s + 2, 0)
-            project(s, 1)
+            if s == -1:
+                for t in range(4):
+                    project(0, t)
             squares(s, 0)
-            gained(s, 0)
-            squares(s, 1)
-            project(s, 2)
-            attend_mm(s - 2, 0)
+            project(s, 1)
             total(s - 1)
-            project(s, 3)
+            quant_z(s - 2)
             inverse_rms(s - 1)
             spread_rms(s - 1)
-            attend_out(s - 2, 0)
-            squares(s, 2)
-            squares(s, 3)
+            gained(s, 0)
+            scale_out(s + 2, 0)
+            attend_mm(s - 2, 0)
+            project(s, 2)
+            squares(s, 1)
             attend_mm(s - 2, 1)
-            scale_out(s + 2, 1)
-            project(s + 1, 0)
             gained(s, 1)
-            turn(s + 3, 0)
+            attend_out(s - 2, 0)
+            project(s, 3)
+            scale_out(s + 2, 1)
             if s == -3:
                 prepare_weights()
-            if s % 2 == 1:
-                quant_k(s // 2)
-            turn(s + 3, 1)
-            if s == -4:
-                cast(s + 4, "v", 0, 2)
-                cast(s + 4, "s", 2, 2)
-            elif s == -3:
-                cast(s + 4, "s", 0, 4)
-            else:
-                for i in range(TILES):
-                    cast(s + 4, "g", i, 1)
+            squares(s, 2)
             if s % 2 == 0:
                 keys(s // 2)
             normalise(s - 1)
-            attend_out(s - 2, 1)
+            squares(s, 3)
+            quant_x(s + 2)
+            turn(s + 3, 0)
             gained(s, 2)
             gained(s, 3)
+            attend_out(s - 2, 1)
+            if s % 2 == 1:
+                quant_k(s // 2)
+            if s == -4:
+                cast(s + 4, 0, "vs")
+            elif s in (-3, -2):
+                cast(s + 4, 0, "ss")
+                cast(s + 4, 1, "ss")
+            else:
+                cast(s + 4, 0, "gg")
+                cast(s + 4, 1, "gg")
+            sum_squares(s)
             if s % 2 == 0:
                 keys_out(s // 2)
-            sum_squares(s)
-            quant_x(s + 2)
-            quant_z(s - 1)
+            project(s + 1, 0)
+            turn(s + 3, 1)

@@ -181,7 +181,7 @@ def tile_crossattention_pb_t_w8_kernel(
             if not has(g):
                 return
             if t == 0:
-                y[g] = sb.tile([P, 4, width(g)], F32, name="y", tag="y", bufs=2)
+                y[g] = sb.tile([P, 4, width(g)], F32, name="y", tag="y", bufs=3)
             nc.scalar.activation(
                 out=y[g][:, t, :],
                 in_=qt[g, t][:],
@@ -304,40 +304,16 @@ def tile_crossattention_pb_t_w8_kernel(
             dst = out[pair // PPB].rearrange("(p i) s -> p i s", i=ROWS)
             nc.sync.dma_start(out=dst[:, i0 : i0 + 2, :], in_=osb[g, h][:])
 
-        for s in range(-4, NG + 3):
+        for s in range(-4, NG + 4):
+            gained(s, 0)
+            project(s, 1)
+            scale_out(s + 2, 0)
+            turn(s + 3, 0)
+            normalise(s - 2)
+            squares(s, 0)
             if s == -1:
                 for t in range(4):
                     project(0, t)
-            squares(s, 0)
-            project(s, 1)
-            total(s - 1)
-            quant_z(s - 2)
-            inverse_rms(s - 1)
-            spread_rms(s - 1)
-            gained(s, 0)
-            scale_out(s + 2, 0)
-            attend_mm(s - 2, 0)
-            project(s, 2)
-            squares(s, 1)
-            attend_mm(s - 2, 1)
-            gained(s, 1)
-            attend_out(s - 2, 0)
-            project(s, 3)
-            scale_out(s + 2, 1)
-            if s == -3:
-                prepare_weights()
-            squares(s, 2)
-            if s % 2 == 0:
-                keys(s // 2)
-            normalise(s - 1)
-            squares(s, 3)
-            quant_x(s + 2)
-            turn(s + 3, 0)
-            gained(s, 2)
-            gained(s, 3)
-            attend_out(s - 2, 1)
-            if s % 2 == 1:
-                quant_k(s // 2)
             if s == -4:
                 cast(s + 4, 0, "vs")
             elif s in (-3, -2):
@@ -345,9 +321,33 @@ def tile_crossattention_pb_t_w8_kernel(
                 cast(s + 4, 1, "ss")
             else:
                 cast(s + 4, 0, "gg")
-                cast(s + 4, 1, "gg")
-            sum_squares(s)
+                cast(s + 4, 1, "gs" if s % 2 else "gg")
+            squares(s, 1)
+            gained(s, 1)
+            total(s - 1)
+            inverse_rms(s - 1)
+            attend_mm(s - 3, 0)
+            attend_mm(s - 3, 1)
+            scale_out(s + 2, 1)
+            quant_z(s - 2)
+            attend_out(s - 3, 0)
+            if s % 2 == 0:
+                keys(s // 2)
+            quant_x(s + 2)
+            project(s, 2)
+            if s == -3:
+                prepare_weights()
+            attend_out(s - 3, 1)
+            project(s, 3)
+            project(s + 1, 0)
+            spread_rms(s - 1)
+            squares(s, 2)
+            turn(s + 3, 1)
+            squares(s, 3)
+            gained(s, 2)
+            gained(s, 3)
             if s % 2 == 0:
                 keys_out(s // 2)
-            project(s + 1, 0)
-            turn(s + 3, 1)
+            if s % 2 == 1:
+                quant_k(s // 2)
+            sum_squares(s)

from contextlib import ExitStack

import concourse.mybir as mybir
from concourse.masks import make_identity

B, T, S, K, F = 8, 1024, 256, 512, 512
EPS = 1e-6
FLOPS = 2 * B * T * K * F + 2 * B * T * F * S

F32 = mybir.dt.float32
BF16 = mybir.dt.bfloat16
I32 = mybir.dt.int32
U32 = mybir.dt.uint32
U8 = mybir.dt.uint8
F8 = mybir.dt.float8_e4m3fn
FP8X4 = mybir.dt.float8_e4m3fn_x4
ALU = mybir.AluOpType
ACT = mybir.ActivationFunctionType
AXIS = mybir.AxisListType

P = 128
PT = 2 * P
NP = B * T // PT
PPB = T // PT
ROWS = T // P
GROUPS = [[0]] + [[i, i + 1] for i in range(1, NP - 1, 2)] + [[NP - 1]]
NG = len(GROUPS)


def tile_crossattention_pb_t_w8_kernel(
    tc, text_bytes, text_scale, w_words, w_scales, w_bias, qn_w, k_norm, out
):
    nc = tc.nc
    with ExitStack() as ctx:
        const = ctx.enter_context(tc.tile_pool(name="const", bufs=1))
        sb = ctx.enter_context(tc.tile_pool(name="sb", bufs=2))
        ps = ctx.enter_context(tc.psum_pool(name="ps", bufs=1))
        ctx.enter_context(tc.manual_schedule())

        tbs, kbs = {}, {}

        def load_text(b, lo, hi):
            if b not in tbs:
                tbs[b] = sb.tile([P, ROWS * K], U8, name="tb", tag="tb", bufs=B)
            src = text_bytes[b].rearrange("(p i) k -> p (i k)", i=ROWS)
            nc.sync.dma_start(out=tbs[b][:, lo:hi], in_=src[:, lo:hi])

        def load_keys(b):
            kbs[b] = sb.tile([P, 2, F], BF16, name="kb", tag="kb", bufs=B)
            nc.sync.dma_start(out=kbs[b][:], in_=k_norm[b].rearrange("(i p) k -> p i k", p=P))

        load_text(0, 0, 2 * K)
        sc = const.tile([P, 1, 2, 2], F32, name="sc")
        nc.sync.dma_start(out=sc[:], in_=text_scale[0].rearrange("q (p u e) -> p q u e", u=2, e=2))
        w_raw = const.tile([P, F], I32, name="w_raw")
        nc.sync.dma_start(out=w_raw[:], in_=w_words[0].rearrange("p n t -> p (n t)").bitcast(I32))
        load_text(0, 2 * K, ROWS * K)
        ws_raw = const.tile([P, F], U8, name="ws_raw", align_bytes=64)
        nc.vector.memset(ws_raw[:].bitcast(I32), 0)
        for q in range(4):
            nc.sync.dma_start(
                out=ws_raw[32 * q : 32 * q + 4, :].bitcast(I32),
                in_=w_scales[0, 4 * q : 4 * q + 4, :].bitcast(I32),
            )
        b16 = const.tile([P, 4], BF16, name="b16")
        nc.sync.dma_start(out=b16[:], in_=w_bias.rearrange("(p t) -> p t", t=4))
        g16 = const.tile([P, 4], BF16, name="g16")
        nc.sync.dma_start(out=g16[:], in_=qn_w.rearrange("(p t) -> p t", t=4))
        load_keys(0)
        for b in range(1, B):
            load_text(b, 0, ROWS * K)
            load_keys(b)

        ident = const.tile([P, P], F32, name="ident")
        make_identity(nc, ident[:])
        eps = const.tile([P, 1], F32, name="eps")
        nc.gpsimd.memset(eps[:], EPS)

        w_codes = const.tile([P, F], I32, name="w_codes", align_bytes=64)
        w_sc = const.tile([P, F], U8, name="w_sc", align_bytes=64)
        b32 = const.tile([P, 4], F32, name="b32")
        g32 = const.tile([P, 4], F32, name="g32")
        bg32 = const.tile([P, 4], F32, name="bg32")

        def prepare_weights():
            nc.vector.tensor_copy(
                out=w_codes[:].rearrange("p (t m) -> p m t", t=4),
                in_=w_raw[:].rearrange("p (m t) -> p m t", t=4),
            )
            nc.vector.tensor_copy(
                out=w_sc[:].rearrange("p (t m) -> p m t", t=4),
                in_=ws_raw[:].rearrange("p (m t) -> p m t", t=4),
            )
            nc.vector.tensor_copy(out=b32[:], in_=b16[:])
            nc.vector.tensor_copy(out=g32[:], in_=g16[:])
            nc.vector.tensor_tensor(out=bg32[:], in0=b32[:], in1=g32[:], op=ALU.mult)

        xb, tp, xg, xc, xs = {}, {}, {}, {}, {}
        qt, y, sq, ss, tot, rstd, rb, zg, zc, zs = {}, {}, {}, {}, {}, {}, {}, {}, {}, {}
        kts, kgs, kc, ks, ot, osb = {}, {}, {}, {}, {}, {}

        def has(g, h=0):
            return 0 <= g < NG and h < len(GROUPS[g])

        def width(g):
            return len(GROUPS[g]) * PT

        def cast(g, h, engines):
            if not has(g, h):
                return
            xb[g, h] = sb.tile([P, 2 * K], BF16, name="xb", tag="xb", bufs=4)
            pair = GROUPS[g][h]
            for j in range(2):
                base = ((pair % PPB) * 2 + j) * K
                src = tbs[pair // PPB][:, base : base + K].bitcast(F8)
                dst = xb[g, h][:, j * K : (j + 1) * K]
                if engines[j] == "v":
                    nc.vector.tensor_copy(out=dst, in_=src)
                elif engines[j] == "s":
                    nc.scalar.copy(out=dst, in_=src)
                else:
                    nc.gpsimd.tensor_copy(out=dst, in_=src)

        def turn(g, h):
            if not has(g, h):
                return
            tp[g, h] = ps.tile([P, 2, PT], F32, name="tp", tag="tp", bufs=2)
            words = xb[g, h][:].bitcast(F32)
            for j in range(2):
                for u in range(2):
                    nc.tensor.transpose(
                        tp[g, h][:, u, j * P : (j + 1) * P],
                        words[:, j * 256 + u : (j + 1) * 256 : 2],
                        ident[:],
                    )

        def scale_out(g, h):
            if not has(g, h):
                return
            if h == 0:
                xg[g] = sb.tile([P, width(g) * 4], BF16, name="xg", tag="xg", bufs=2, align_bytes=64)
            nc.vector.tensor_tensor(
                out=xg[g][:, h * PT * 4 : (h + 1) * PT * 4].rearrange("p (r u e) -> p r u e", u=2, e=2),
                in0=tp[g, h][:].bitcast(BF16).rearrange("p u (r e) -> p r u e", e=2),
                in1=sc[:].to_broadcast([P, PT, 2, 2]),
                op=ALU.mult,
            )

        def quant_x(g):
            if not has(g):
                return
            xc[g] = sb.tile([P, width(g)], U32, name="xc", tag="xc", bufs=3, align_bytes=64)
            xs[g] = sb.tile([P, width(g)], U8, name="xs", tag="xs", bufs=3, align_bytes=64)
            nc.vector.quantize_mx(out=xc[g][:].bitcast(FP8X4), scales=xs[g][:], in_=xg[g][:])

        def project(g, t):
            if not has(g) or (g, t) in qt:
                return
            qt[g, t] = ps.tile([P, width(g)], F32, name="q", tag="q", bufs=4)
            cols = slice(t * P, (t + 1) * P)
            nc.tensor.matmul_mx(
                out=qt[g, t][:],
                lhsT=w_codes[:, cols].bitcast(FP8X4),
                lhsT_scale=w_sc[:, cols],
                rhs=xc[g][:].bitcast(FP8X4),
                rhs_scale=xs[g][:],
                start=True,
                stop=True,
            )

        def squares(g, t):
            if not has(g):
                return
            if t == 0:
                sq[g] = sb.tile([P, 4, width(g)], F32, name="sq", tag="sq", bufs=2)
            nc.scalar.activation(
                out=sq[g][:, t, :], in_=qt[g, t][:], func=ACT.Square, bias=b32[:, t : t + 1]
            )

        def gained(g, t):
            if not has(g):
                return
            if t == 0:
                y[g] = sb.tile([P, 4, width(g)], F32, name="y", tag="y", bufs=3)
            nc.scalar.activation(
                out=y[g][:, t, :],
                in_=qt[g, t][:],
                func=ACT.Identity,
                bias=bg32[:, t : t + 1],
                scale=g32[:, t : t + 1],
            )

        def sum_squares(g):
            if not has(g):
                return
            tiles = width(g) // P
            ss[g] = ps.tile([P, tiles, P], F32, name="ss", tag="ss", bufs=1)
            for j in range(tiles):
                for t in range(4):
                    nc.tensor.matmul(
                        ss[g][:, j, :],
                        lhsT=sq[g][:, t, j * P : (j + 1) * P],
                        rhs=ident[:],
                        start=(t == 0),
                        stop=(t == 3),
                        is_transpose=True,
                    )

        def total(g):
            if not has(g):
                return
            tot[g] = sb.tile([P, width(g) // P], F32, name="tot", tag="tot", bufs=2)
            nc.vector.tensor_reduce(out=tot[g][:], in_=ss[g][:], axis=AXIS.X, op=ALU.add)

        def inverse_rms(g):
            if not has(g):
                return
            rstd[g] = sb.tile([P, width(g) // P], F32, name="rstd", tag="rstd", bufs=2)
            nc.scalar.activation(
                out=rstd[g][:], in_=tot[g][:], func=ACT.Abs_reciprocal_sqrt, bias=eps[:], scale=1.0 / F
            )

        def spread_rms(g):
            if not has(g):
                return
            rb[g] = ps.tile([P, width(g) // 4, 1, 4], F32, name="rb", tag="rb", bufs=1)
            row = rb[g][:].rearrange("p c o i -> p (c o i)")
            for j in range(width(g) // P):
                nc.tensor.transpose(
                    row[:, j * P : (j + 1) * P], rstd[g][:, j : j + 1].to_broadcast([P, P]), ident[:]
                )

        def normalise(g):
            if not has(g):
                return
            zg[g] = sb.tile([P, width(g) * 4], BF16, name="zg", tag="zg", bufs=2, align_bytes=64)
            nc.vector.tensor_tensor(
                out=zg[g][:].rearrange("p (c i t) -> p c t i", i=4, t=4),
                in0=y[g][:].rearrange("p t (c i) -> p c t i", i=4),
                in1=rb[g][:].to_broadcast([P, width(g) // 4, 4, 4]),
                op=ALU.mult,
            )

        def quant_z(g):
            if not has(g):
                return
            zc[g] = sb.tile([P, width(g)], U32, name="zc", tag="zc", bufs=3, align_bytes=64)
            zs[g] = sb.tile([P, width(g)], U8, name="zs", tag="zs", bufs=3, align_bytes=64)
            nc.vector.quantize_mx(out=zc[g][:].bitcast(FP8X4), scales=zs[g][:], in_=zg[g][:])

        def keys(b):
            if not 0 <= b < B:
                return
            kts[b] = ps.tile([P, 2, S], F32, name="kt", tag="q", bufs=4)
            words = kbs[b][:].rearrange("p i k -> p (i k)").bitcast(F32)
            for i in range(2):
                for u in range(2):
                    nc.tensor.transpose(
                        kts[b][:, u, i * P : (i + 1) * P],
                        words[:, i * 256 + u : (i + 1) * 256 : 2],
                        ident[:],
                    )

        def keys_out(b):
            if not 0 <= b < B:
                return
            kgs[b] = sb.tile([P, S * 4], BF16, name="kg", tag="kg", bufs=2, align_bytes=64)
            nc.scalar.copy(
                out=kgs[b][:].bitcast(F32).rearrange("p (r u) -> p r u", u=2),
                in_=kts[b][:].rearrange("p u r -> p r u"),
            )

        def quant_k(b):
            if not 0 <= b < B:
                return
            kc[b] = sb.tile([P, S], U32, name="kc", tag="kc", bufs=3, align_bytes=64)
            ks[b] = sb.tile([P, S], U8, name="ks", tag="ks", bufs=3, align_bytes=64)
            nc.vector.quantize_mx(out=kc[b][:].bitcast(FP8X4), scales=ks[b][:], in_=kgs[b][:])

        def attend_mm(g, h):
            if not has(g, h):
                return
            b = GROUPS[g][h] // PPB
            ot[g, h] = ps.tile([P, 2, S], F32, name="o", tag="q", bufs=4)
            for j in range(2):
                cols = slice((2 * h + j) * P, (2 * h + j + 1) * P)
                nc.tensor.matmul_mx(
                    out=ot[g, h][:, j, :],
                    lhsT=zc[g][:, cols].bitcast(FP8X4),
                    lhsT_scale=zs[g][:, cols],
                    rhs=kc[b][:].bitcast(FP8X4),
                    rhs_scale=ks[b][:],
                    start=True,
                    stop=True,
                )

        def attend_out(g, h):
            if not has(g, h):
                return
            pair = GROUPS[g][h]
            osb[g, h] = sb.tile([P, 2, S], F32, name="osb", tag="osb", bufs=6)
            nc.scalar.activation(out=osb[g, h][:], in_=ot[g, h][:], func=ACT.Copy, scale=F**-0.5)
            i0 = (pair % PPB) * 2
            dst = out[pair // PPB].rearrange("(p i) s -> p i s", i=ROWS)
            nc.sync.dma_start(out=dst[:, i0 : i0 + 2, :], in_=osb[g, h][:])

        for s in range(-4, NG + 4):
            gained(s, 0)
            project(s, 1)
            scale_out(s + 2, 0)
            turn(s + 3, 0)
            normalise(s - 2)
            squares(s, 0)
            if s == -1:
                for t in range(4):
                    project(0, t)
            if s == -4:
                cast(s + 4, 0, "vs")
            elif s in (-3, -2):
                cast(s + 4, 0, "ss")
                cast(s + 4, 1, "ss")
            else:
                cast(s + 4, 0, "gg")
                cast(s + 4, 1, "gs" if s % 2 else "gg")
            squares(s, 1)
            gained(s, 1)
            total(s - 1)
            inverse_rms(s - 1)
            attend_mm(s - 3, 0)
            attend_mm(s - 3, 1)
            scale_out(s + 2, 1)
            quant_z(s - 2)
            attend_out(s - 3, 0)
            if s % 2 == 0:
                keys(s // 2)
            quant_x(s + 2)
            project(s, 2)
            if s == -3:
                prepare_weights()
            attend_out(s - 3, 1)
            project(s, 3)
            project(s + 1, 0)
            spread_rms(s - 1)
            squares(s, 2)
            turn(s + 3, 1)
            squares(s, 3)
            gained(s, 2)
            gained(s, 3)
            if s % 2 == 0:
                keys_out(s // 2)
            if s % 2 == 1:
                quant_k(s // 2)
            sum_squares(s)
